import numpy as np
import ml_dtypes

BF16 = ml_dtypes.bfloat16


def bf(x):
    return np.asarray(x, np.float32).astype(BF16)


def f32(x):
    return np.asarray(x, np.float32)


def f64(x):
    return np.asarray(x).astype(np.float64)


def striped(idx):
    return np.tile(idx.reshape(-1, 16).T, (8, 1))


D, S, N, MAXF, TMAX, DMAX = 384, 256, 64, 20, 30, 1000


def setup_inputs():
    return {"emb": f32(np.random.standard_normal((D, S))), "tfs": f32(1 + np.random.choice(TMAX, size=(1, N))), "dfs": f32(1 + np.random.choice(DMAX, size=(1, N))), "offs": striped(np.random.permutation(np.tile(np.arange(S), 2))[:N])}


def reference(emb, tfs, dfs, offs):
    idx = offs[:16].T.reshape(-1)
    tf = np.log(1.0 + np.minimum(f64(tfs), MAXF))
    idf = 1.0 / np.log(f64(dfs) + 2.0)
    return f64(emb)[:, idx] * (tf * idf)

@@ -1,0 +1,44 @@
+import concourse.mybir as mybir
+
+P = 128
+CHANNELS, WORDS, TOKENS = 384, 256, 64
+BLOCKS = CHANNELS // P
+MAX_TF = 20.0
+
+F32, U16 = mybir.dt.float32, mybir.dt.uint16
+ALU = mybir.AluOpType
+LN = mybir.ActivationFunctionType.Ln
+
+
+def tile_attentiontfidf_kernel(tc, emb, tfs, dfs, offs, out):
+    nc = tc.nc
+    with tc.tile_pool(name="held", bufs=1) as held:
+        offsets = held.tile([P, TOKENS // 16], U16, name="offsets")
+        nc.sync.dma_start(offsets[:], offs)
+
+        df = held.tile([P, TOKENS], F32, name="df")
+        tf = held.tile([P, TOKENS], F32, name="tf")
+        nc.scalar.dma_start(df[:], dfs.broadcast_to([P, TOKENS]))
+        nc.scalar.dma_start(tf[:], tfs.broadcast_to([P, TOKENS]))
+
+        tables = [held.tile([P, WORDS], F32, name=f"table{b}") for b in range(BLOCKS)]
+        for b in range(BLOCKS):
+            nc.sync.dma_start(tables[b][:], emb[b * P : (b + 1) * P, :])
+
+        log_df = held.tile([P, TOKENS], F32, name="log_df")
+        nc.scalar.activation(log_df[:], df[:], LN, bias=2.0)
+        idf = held.tile([P, TOKENS], F32, name="idf")
+        nc.vector.reciprocal(idf[:], log_df[:])
+
+        clipped = held.tile([P, TOKENS], F32, name="clipped")
+        nc.vector.tensor_scalar_min(clipped[:], tf[:], MAX_TF)
+        damped = held.tile([P, TOKENS], F32, name="damped")
+        nc.scalar.activation(damped[:], clipped[:], LN, bias=1.0)
+
+        wt = held.tile([P, TOKENS], F32, name="wt")
+        nc.vector.tensor_tensor(wt[:], damped[:], idf[:], ALU.mult)
+
+        for b in range(BLOCKS):
+            weighted = held.tile([P, TOKENS], F32, name=f"weighted{b}")
+            nc.vector.tensor_tensor(weighted[:], tables[b][:].indirect(offsets[:]), wt[:], ALU.mult)
+            nc.sync.dma_start(out[b * P : (b + 1) * P, :], weighted[:])

@@ -19,11 +19,11 @@ def tile_attentiontfidf_kernel(tc, emb, tfs, dfs, offs, out):
         df = held.tile([P, TOKENS], F32, name="df")
         tf = held.tile([P, TOKENS], F32, name="tf")
         nc.scalar.dma_start(df[:], dfs.broadcast_to([P, TOKENS]))
-        nc.scalar.dma_start(tf[:], tfs.broadcast_to([P, TOKENS]))
+        nc.gpsimd.dma_start(tf[:], tfs.broadcast_to([P, TOKENS]))
 
         tables = [held.tile([P, WORDS], F32, name=f"table{b}") for b in range(BLOCKS)]
-        for b in range(BLOCKS):
-            nc.sync.dma_start(tables[b][:], emb[b * P : (b + 1) * P, :])
+        for b, queue in enumerate((nc.sync, nc.scalar, nc.gpsimd)):
+            queue.dma_start(tables[b][:], emb[b * P : (b + 1) * P, :])
 
         log_df = held.tile([P, TOKENS], F32, name="log_df")
         nc.scalar.activation(log_df[:], df[:], LN, bias=2.0)

@@ -14,16 +14,16 @@ def tile_attentiontfidf_kernel(tc, emb, tfs, dfs, offs, out):
     nc = tc.nc
     with tc.tile_pool(name="held", bufs=1) as held:
         offsets = held.tile([P, TOKENS // 16], U16, name="offsets")
-        nc.sync.dma_start(offsets[:], offs)
 
         df = held.tile([P, TOKENS], F32, name="df")
         tf = held.tile([P, TOKENS], F32, name="tf")
-        nc.scalar.dma_start(df[:], dfs.broadcast_to([P, TOKENS]))
-        nc.gpsimd.dma_start(tf[:], tfs.broadcast_to([P, TOKENS]))
+        nc.sync.dma_start(df[:], dfs.broadcast_to([P, TOKENS]))
+        nc.scalar.dma_start(tf[:], tfs.broadcast_to([P, TOKENS]))
+        nc.sync.dma_start(offsets[:], offs)
 
         tables = [held.tile([P, WORDS], F32, name=f"table{b}") for b in range(BLOCKS)]
-        for b, queue in enumerate((nc.sync, nc.scalar, nc.gpsimd)):
-            queue.dma_start(tables[b][:], emb[b * P : (b + 1) * P, :])
+        for b in range(BLOCKS):
+            nc.sync.dma_start(tables[b][:], emb[b * P : (b + 1) * P, :])
 
         log_df = held.tile([P, TOKENS], F32, name="log_df")
         nc.scalar.activation(log_df[:], df[:], LN, bias=2.0)

@@ -38,7 +38,7 @@ def tile_attentiontfidf_kernel(tc, emb, tfs, dfs, offs, out):
         wt = held.tile([P, TOKENS], F32, name="wt")
         nc.vector.tensor_tensor(wt[:], damped[:], idf[:], ALU.mult)
 
+        weighted = held.tile([P, BLOCKS, TOKENS], F32, name="weighted")
         for b in range(BLOCKS):
-            weighted = held.tile([P, TOKENS], F32, name=f"weighted{b}")
-            nc.vector.tensor_tensor(weighted[:], tables[b][:].indirect(offsets[:]), wt[:], ALU.mult)
-            nc.sync.dma_start(out[b * P : (b + 1) * P, :], weighted[:])
+            nc.vector.tensor_tensor(weighted[:, b, :], tables[b][:].indirect(offsets[:]), wt[:], ALU.mult)
+        nc.sync.dma_start(out.rearrange("(b p) j -> p b j", p=P), weighted[:])

@@ -18,7 +18,7 @@ def tile_attentiontfidf_kernel(tc, emb, tfs, dfs, offs, out):
         df = held.tile([P, TOKENS], F32, name="df")
         tf = held.tile([P, TOKENS], F32, name="tf")
         nc.sync.dma_start(df[:], dfs.broadcast_to([P, TOKENS]))
-        nc.scalar.dma_start(tf[:], tfs.broadcast_to([P, TOKENS]))
+        nc.sync.dma_start(tf[:], tfs.broadcast_to([P, TOKENS]))
         nc.sync.dma_start(offsets[:], offs)
 
         tables = [held.tile([P, WORDS], F32, name=f"table{b}") for b in range(BLOCKS)]

@@ -18,12 +18,13 @@ def tile_attentiontfidf_kernel(tc, emb, tfs, dfs, offs, out):
         df = held.tile([P, TOKENS], F32, name="df")
         tf = held.tile([P, TOKENS], F32, name="tf")
         nc.sync.dma_start(df[:], dfs.broadcast_to([P, TOKENS]))
-        nc.sync.dma_start(tf[:], tfs.broadcast_to([P, TOKENS]))
+        nc.scalar.dma_start(tf[:], tfs.broadcast_to([P, TOKENS]))
         nc.sync.dma_start(offsets[:], offs)
 
+        emb_blocks = emb.rearrange("(p b) w -> b p w", b=BLOCKS)
         tables = [held.tile([P, WORDS], F32, name=f"table{b}") for b in range(BLOCKS)]
         for b in range(BLOCKS):
-            nc.sync.dma_start(tables[b][:], emb[b * P : (b + 1) * P, :])
+            nc.sync.dma_start(tables[b][:], emb_blocks[b])
 
         log_df = held.tile([P, TOKENS], F32, name="log_df")
         nc.scalar.activation(log_df[:], df[:], LN, bias=2.0)
@@ -41,4 +42,4 @@ def tile_attentiontfidf_kernel(tc, emb, tfs, dfs, offs, out):
         weighted = held.tile([P, BLOCKS, TOKENS], F32, name="weighted")
         for b in range(BLOCKS):
             nc.vector.tensor_tensor(weighted[:, b, :], tables[b][:].indirect(offsets[:]), wt[:], ALU.mult)
-        nc.sync.dma_start(out.rearrange("(b p) j -> p b j", p=P), weighted[:])
+        nc.sync.dma_start(out.rearrange("(p b) j -> p b j", b=BLOCKS), weighted[:])

@@ -1,9 +1,12 @@
+import math
+
 import concourse.mybir as mybir
 
 P = 128
 CHANNELS, WORDS, TOKENS = 384, 256, 64
 BLOCKS = CHANNELS // P
 MAX_TF = 20.0
+MAX_DAMPED = math.log(1.0 + MAX_TF)
 
 F32, U16 = mybir.dt.float32, mybir.dt.uint16
 ALU = mybir.AluOpType
@@ -28,16 +31,14 @@ def tile_attentiontfidf_kernel(tc, emb, tfs, dfs, offs, out):
 
         log_df = held.tile([P, TOKENS], F32, name="log_df")
         nc.scalar.activation(log_df[:], df[:], LN, bias=2.0)
+        log_tf = held.tile([P, TOKENS], F32, name="log_tf")
+        nc.scalar.activation(log_tf[:], tf[:], LN, bias=1.0)
+
         idf = held.tile([P, TOKENS], F32, name="idf")
         nc.vector.reciprocal(idf[:], log_df[:])
 
-        clipped = held.tile([P, TOKENS], F32, name="clipped")
-        nc.vector.tensor_scalar_min(clipped[:], tf[:], MAX_TF)
-        damped = held.tile([P, TOKENS], F32, name="damped")
-        nc.scalar.activation(damped[:], clipped[:], LN, bias=1.0)
-
         wt = held.tile([P, TOKENS], F32, name="wt")
-        nc.vector.tensor_tensor(wt[:], damped[:], idf[:], ALU.mult)
+        nc.vector.scalar_tensor_tensor(wt[:], log_tf[:], MAX_DAMPED, idf[:], ALU.min, ALU.mult)
 
         weighted = held.tile([P, BLOCKS, TOKENS], F32, name="weighted")
         for b in range(BLOCKS):

@@ -37,8 +37,11 @@ def tile_attentiontfidf_kernel(tc, emb, tfs, dfs, offs, out):
         idf = held.tile([P, TOKENS], F32, name="idf")
         nc.vector.reciprocal(idf[:], log_df[:])
 
+        damped = held.tile([P, TOKENS], F32, name="damped")
+        nc.vector.tensor_scalar_min(damped[:], log_tf[:], MAX_DAMPED)
+
         wt = held.tile([P, TOKENS], F32, name="wt")
-        nc.vector.scalar_tensor_tensor(wt[:], log_tf[:], MAX_DAMPED, idf[:], ALU.min, ALU.mult)
+        nc.vector.tensor_tensor(wt[:], damped[:], idf[:], ALU.mult)
 
         weighted = held.tile([P, BLOCKS, TOKENS], F32, name="weighted")
         for b in range(BLOCKS):

@@ -30,18 +30,22 @@ def tile_attentiontfidf_kernel(tc, emb, tfs, dfs, offs, out):
             nc.sync.dma_start(tables[b][:], emb_blocks[b])
 
         log_df = held.tile([P, TOKENS], F32, name="log_df")
-        nc.scalar.activation(log_df[:], df[:], LN, bias=2.0)
+        halves = [slice(0, TOKENS // 2), slice(TOKENS // 2, TOKENS)]
+        for half in halves:
+            nc.scalar.activation(log_df[:, half], df[:, half], LN, bias=2.0)
         log_tf = held.tile([P, TOKENS], F32, name="log_tf")
         nc.scalar.activation(log_tf[:], tf[:], LN, bias=1.0)
 
         idf = held.tile([P, TOKENS], F32, name="idf")
-        nc.vector.reciprocal(idf[:], log_df[:])
-
         damped = held.tile([P, TOKENS], F32, name="damped")
-        nc.vector.tensor_scalar_min(damped[:], log_tf[:], MAX_DAMPED)
-
         wt = held.tile([P, TOKENS], F32, name="wt")
-        nc.vector.tensor_tensor(wt[:], damped[:], idf[:], ALU.mult)
+
+        nc.vector.reciprocal(idf[:, halves[0]], log_df[:, halves[0]])
+        nc.vector.tensor_scalar_min(damped[:], log_tf[:], MAX_DAMPED)
+        nc.vector.reciprocal(idf[:, halves[1]], log_df[:, halves[1]])
+
+        for half in halves:
+            nc.vector.tensor_tensor(wt[:, half], damped[:, half], idf[:, half], ALU.mult)
 
         weighted = held.tile([P, BLOCKS, TOKENS], F32, name="weighted")
         for b in range(BLOCKS):

@@ -50,4 +50,7 @@ def tile_attentiontfidf_kernel(tc, emb, tfs, dfs, offs, out):
         weighted = held.tile([P, BLOCKS, TOKENS], F32, name="weighted")
         for b in range(BLOCKS):
             nc.vector.tensor_tensor(weighted[:, b, :], tables[b][:].indirect(offsets[:]), wt[:], ALU.mult)
-        nc.sync.dma_start(out.rearrange("(p b) j -> p b j", b=BLOCKS), weighted[:])
+
+        out_blocks = out.rearrange("(p b) j -> p b j", b=BLOCKS)
+        nc.scalar.dma_start(out_blocks[:, : BLOCKS - 1, :], weighted[:, : BLOCKS - 1, :])
+        nc.sync.dma_start(out_blocks[:, BLOCKS - 1, :], weighted[:, BLOCKS - 1, :])

import math

import concourse.mybir as mybir

P = 128
CHANNELS, WORDS, TOKENS = 384, 256, 64
BLOCKS = CHANNELS // P
MAX_TF = 20.0
MAX_DAMPED = math.log(1.0 + MAX_TF)

F32, U16 = mybir.dt.float32, mybir.dt.uint16
ALU = mybir.AluOpType
LN = mybir.ActivationFunctionType.Ln


def tile_attentiontfidf_kernel(tc, emb, tfs, dfs, offs, out):
    nc = tc.nc
    with tc.tile_pool(name="held", bufs=1) as held:
        offsets = held.tile([P, TOKENS // 16], U16, name="offsets")

        df = held.tile([P, TOKENS], F32, name="df")
        tf = held.tile([P, TOKENS], F32, name="tf")
        nc.sync.dma_start(df[:], dfs.broadcast_to([P, TOKENS]))
        nc.scalar.dma_start(tf[:], tfs.broadcast_to([P, TOKENS]))
        nc.sync.dma_start(offsets[:], offs)

        emb_blocks = emb.rearrange("(p b) w -> b p w", b=BLOCKS)
        tables = [held.tile([P, WORDS], F32, name=f"table{b}") for b in range(BLOCKS)]
        for b in range(BLOCKS):
            nc.sync.dma_start(tables[b][:], emb_blocks[b])

        log_df = held.tile([P, TOKENS], F32, name="log_df")
        halves = [slice(0, TOKENS // 2), slice(TOKENS // 2, TOKENS)]
        for half in halves:
            nc.scalar.activation(log_df[:, half], df[:, half], LN, bias=2.0)
        log_tf = held.tile([P, TOKENS], F32, name="log_tf")
        nc.scalar.activation(log_tf[:], tf[:], LN, bias=1.0)

        idf = held.tile([P, TOKENS], F32, name="idf")
        damped = held.tile([P, TOKENS], F32, name="damped")
        wt = held.tile([P, TOKENS], F32, name="wt")

        nc.vector.reciprocal(idf[:, halves[0]], log_df[:, halves[0]])
        nc.vector.tensor_scalar_min(damped[:], log_tf[:], MAX_DAMPED)
        nc.vector.reciprocal(idf[:, halves[1]], log_df[:, halves[1]])

        for half in halves:
            nc.vector.tensor_tensor(wt[:, half], damped[:, half], idf[:, half], ALU.mult)

        weighted = held.tile([P, BLOCKS, TOKENS], F32, name="weighted")
        for b in range(BLOCKS):
            nc.vector.tensor_tensor(weighted[:, b, :], tables[b][:].indirect(offsets[:]), wt[:], ALU.mult)

        out_blocks = out.rearrange("(p b) j -> p b j", b=BLOCKS)
        nc.scalar.dma_start(out_blocks[:, : BLOCKS - 1, :], weighted[:, : BLOCKS - 1, :])
        nc.sync.dma_start(out_blocks[:, BLOCKS - 1, :], weighted[:, BLOCKS - 1, :])
